import numpy as np
import ml_dtypes


def mxq(x, axis, fmt="e4m3"):
    dtype, down = {"e4m3": (ml_dtypes.float8_e4m3fn, 7), "e5m2": (ml_dtypes.float8_e5m2, 14)}[fmt]
    v = np.moveaxis(np.asarray(x, np.float32).astype(ml_dtypes.bfloat16).astype(np.float64), axis, -1)
    blocks = v.reshape(v.shape[:-1] + (-1, 32))
    amax = np.abs(blocks).max(-1, keepdims=True)
    byte = np.maximum(np.where(amax > 0, np.frexp(amax)[1] - 1 + 127, 0) - down, 1)
    scale = np.exp2(byte - 127.0)
    codes = (blocks / scale).astype(np.float32).astype(dtype).astype(np.float64)
    return np.moveaxis((codes * scale).reshape(v.shape), -1, axis)


WIDE = False


def mx_kscale(k):
    if not WIDE:
        return np.ones(k)
    levels = np.array([10, -10, 5, -5, 0])
    if k % 512:
        return np.exp2(np.random.permutation(np.resize(levels, k // 32))).repeat(32)
    a = np.empty((k // 512, 16))
    for p in range(k // 512):
        a[p, :8] = np.random.permutation(np.resize(levels, 8))
        for g in range(8):
            far = levels[np.abs(levels - a[p, g]) >= 10]
            a[p, g + 8] = far[np.random.randint(len(far))]
    return np.exp2(a.ravel()).repeat(32)


BF16 = ml_dtypes.bfloat16


def bf(x):
    return np.asarray(x, np.float32).astype(BF16)


def f64(x):
    return np.asarray(x).astype(np.float64)


B, LQ, N, LD, D = 4, 32, 16, 512, 512

EPS = 1e-12


def _l2norm(x):
    n = np.sqrt(np.sum(x * x, axis=-1, keepdims=True))
    return x / np.maximum(n, EPS)


def setup_inputs():
    s = mx_kscale(D)
    c1 = np.exp2(np.round(np.log2(np.sqrt(np.mean(s * s)))))
    c2 = np.exp2(np.round(np.log2(np.sqrt(np.mean(1.0 / (s * s))))))
    x1 = np.random.standard_normal((B, LQ, D)) * s * (np.random.random((B, LQ, 1)) >= 0.0625)
    x2 = np.random.standard_normal((B, N, LD, D)) / s * (np.random.random((B, N, LD, 1)) >= 0.0625)
    x1_mask = (np.random.random((B, LQ)) >= 0.25) * c1
    x2_mask = (np.random.random((B, N, LD)) >= 0.5) * c2
    return {'x1': bf(x1), 'x2': bf(x2), 'x1_mask': bf(x1_mask), 'x2_mask': bf(x2_mask)}


def reference(x1, x2, x1_mask, x2_mask):
    a = _l2norm(f64(x1)) * f64(x1_mask)[..., None]
    d = _l2norm(f64(x2)) * f64(x2_mask)[..., None]
    sim = mxq(a, 2, 'e4m3')[:, None] @ mxq(d, 3, 'e4m3').transpose(0, 1, 3, 2)
    return sim.max(axis=-1).sum(axis=-1)

@@ -1,0 +1,289 @@
+from contextlib import ExitStack
+
+import concourse.mybir as mybir
+from concourse.masks import make_identity
+
+F32 = mybir.dt.float32
+BF16 = mybir.dt.bfloat16
+U8 = mybir.dt.uint8
+U32 = mybir.dt.uint32
+I32 = mybir.dt.int32
+FP8X4 = mybir.dt.float8_e4m3fn_x4
+ACT = mybir.ActivationFunctionType
+ALU = mybir.AluOpType
+AX = mybir.AxisListType
+
+P = 128
+NB = 4
+ND = 16
+LQ = 32
+LD = 512
+D = 512
+DOCS = NB * ND
+TOK = 4
+LIFT = 128.0
+TINY = 8e-27
+GUARD = 1e12 / LIFT
+
+FLOPS = 2 * NB * ND * LQ * LD * D
+
+GROUP_SIZES = [1, 1] + [2] * 31
+XR_BUFS = 14
+CLOCK_PASSES = 1
+SCALAR_SHARE = 8
+TAIL = 3
+
+
+def tile_lateinteraction_kernel(tc, x1, x2, x1_mask, x2_mask, out):
+    nc = tc.nc
+    first = []
+    group_of = []
+    for g, size in enumerate(GROUP_SIZES):
+        first.append(len(group_of))
+        group_of.extend([g] * size)
+    groups = len(GROUP_SIZES)
+
+    with ExitStack() as ctx:
+        const = ctx.enter_context(tc.tile_pool(name="const", bufs=1))
+        xr_pool = ctx.enter_context(tc.tile_pool(name="xr", bufs=XR_BUFS))
+        work = ctx.enter_context(tc.tile_pool(name="work", bufs=3))
+        junk_pool = ctx.enter_context(tc.tile_pool(name="junk", bufs=4))
+        tp_pool = ctx.enter_context(tc.psum_pool(name="tp", bufs=4))
+        acc_pool = ctx.enter_context(tc.psum_pool(name="acc", bufs=2))
+        misc_pool = ctx.enter_context(tc.psum_pool(name="misc", bufs=1))
+        ctx.enter_context(tc.manual_schedule())
+
+        ident = const.tile([P, P], BF16, name="ident")
+        identf = const.tile([P, P], F32, name="identf")
+        blkm = const.tile([P, P], F32, name="blkm")
+        tiny = const.tile([P, 1], F32, name="tiny")
+        warm = const.tile([P, 1], F32, name="warm")
+        ss_all = const.tile([P, DOCS * TOK], F32, name="ss_all")
+        nr_all = const.tile([P, DOCS * TOK], F32, name="nr_all")
+        rm_all = const.tile([P, DOCS * TOK], F32, name="rm_all")
+        mk = const.tile([P, DOCS * TOK], F32, name="mk")
+        mrow = const.tile([P, LD], BF16, name="mrow")
+        mx = const.tile([P, ND], F32, name="mx")
+        res = const.tile([P, ND], F32, name="res")
+        xq = const.tile([P, D], BF16, name="xq")
+        aq = const.tile([P, D], BF16, name="aq")
+        junkq = const.tile([P, D], BF16, name="junkq")
+        mq_bf = const.tile([P, 1], BF16, name="mq_bf")
+        mq = const.tile([P, 1], F32, name="mq")
+        ssq = const.tile([P, 1], F32, name="ssq")
+        nrq = const.tile([P, 1], F32, name="nrq")
+        rmq = const.tile([P, 1], F32, name="rmq")
+        ga4 = const.tile([P, NB * P * 4], BF16, name="ga4", align_bytes=64)
+        a_codes = const.tile([P, NB * P], U32, name="a_codes", align_bytes=64)
+        a_scl = const.tile([P, NB * P], U8, name="a_scl", align_bytes=64)
+
+        xr_t = {}
+        xs_t = {}
+        pt_t = {}
+        gr_t = {}
+        cd_t = {}
+        sc_t = {}
+        acc_t = {}
+        spare = {}
+        state = {"loads": 0, "b_done": 0, "act": 0}
+
+        def doc_bn(i):
+            return i % NB, i // NB
+
+        def cols_of(g):
+            return slice(first[g] * TOK, (first[g] + GROUP_SIZES[g]) * TOK)
+
+        def pump_loads():
+            while state["loads"] < min(DOCS, state["b_done"] + XR_BUFS):
+                i = state["loads"]
+                b, n = doc_bn(i)
+                t = xr_pool.tile([P, TOK, D], BF16, name="xr")
+                nc.sync.dma_start(out=t[:], in_=x2[b, n].rearrange("(p c) f -> p c f", c=TOK))
+                xr_t[i] = t
+                state["loads"] = i + 1
+
+        def sumsq(i, c):
+            junk = junk_pool.tile([P, D], BF16, name="junk")
+            col = i * TOK + c
+            nc.scalar.activation(out=junk[:], in_=xr_t[i][:, c, :], func=ACT.Square, accum_out=ss_all[:, col : col + 1])
+
+        def inv_norm(g):
+            cols = cols_of(g)
+            nc.scalar.activation(out=nr_all[:, cols], in_=ss_all[:, cols], func=ACT.Abs_reciprocal_sqrt, bias=tiny[:], scale=LIFT * LIFT)
+
+        def row_factor(g):
+            cols = cols_of(g)
+            nc.vector.scalar_tensor_tensor(
+                out=rm_all[:, cols], in0=nr_all[:, cols], scalar=GUARD, in1=mk[:, cols], op0=ALU.min, op1=ALU.mult
+            )
+
+        def scaled(out, in_, factor):
+            nc.vector.tensor_scalar(
+                out=out.rearrange("p (u g e) -> p u g e", u=2, e=16),
+                in0=in_.rearrange("p (g u e) -> p u g e", u=2, e=16),
+                scalar1=factor,
+                scalar2=None,
+                op0=ALU.mult,
+            )
+
+        def scale_rows(i):
+            xs = work.tile([P, TOK, D], BF16, name="xs")
+            for c in range(TOK):
+                col = i * TOK + c
+                scaled(xs[:, c, :], xr_t[i][:, c, :], rm_all[:, col : col + 1])
+            xs_t[i] = xs
+            state["b_done"] = i + 1
+
+        def transposes(i):
+            for hb in range(2):
+                pt = tp_pool.tile([P, 2, 2, P], F32, name="pt")
+                for cc in range(2):
+                    words = xs_t[i][:, 2 * hb + cc, :].bitcast(F32)
+                    for u in range(2):
+                        nc.tensor.transpose(pt[:, cc, u, :], words[:, u * P : (u + 1) * P], identf[:])
+                pt_t[(i, hb)] = pt
+
+        def evacuate(i):
+            gr = work.tile([P, 4 * LD], BF16, name="gr", align_bytes=64)
+            for hb in range(2):
+                dst = gr[:, hb * 1024 : (hb + 1) * 1024].bitcast(F32).rearrange("p (c r u) -> p c r u", c=2, u=2)
+                src = pt_t[(i, hb)][:].rearrange("p c u r -> p c r u")
+                on_scalar = hb == 1 and (i % SCALAR_SHARE == SCALAR_SHARE - 1 or i >= DOCS - TAIL)
+                if on_scalar:
+                    nc.scalar.copy(out=dst, in_=src)
+                else:
+                    nc.vector.tensor_copy(out=dst, in_=src)
+            gr_t[i] = gr
+
+        def quantise(i):
+            cd = work.tile([P, LD], U32, name="cd", align_bytes=64)
+            sc = work.tile([P, LD], U8, name="sc", align_bytes=64)
+            nc.vector.quantize_mx(out=cd[:].bitcast(FP8X4), scales=sc[:], in_=gr_t[i][:])
+            cd_t[i] = cd
+            sc_t[i] = sc
+
+        def product(i):
+            b, n = doc_bn(i)
+            if b == 0:
+                acc_t[n] = acc_pool.tile([P, LD], F32, name="acc")
+            bs = slice(b * P, (b + 1) * P)
+            nc.tensor.matmul_mx(
+                out=acc_t[n][:],
+                lhsT=a_codes[:, bs].bitcast(FP8X4),
+                lhsT_scale=a_scl[:, bs],
+                rhs=cd_t[i][:].bitcast(FP8X4),
+                rhs_scale=sc_t[i][:],
+                start=(b == 0),
+                stop=(b == NB - 1),
+            )
+            for r in range(CLOCK_PASSES):
+                nc.tensor.matmul_mx(
+                    out=spare["t"][:],
+                    lhsT=a_codes[:, bs].bitcast(FP8X4),
+                    lhsT_scale=a_scl[:, bs],
+                    rhs=cd_t[i][:].bitcast(FP8X4),
+                    rhs_scale=sc_t[i][:],
+                    start=True,
+                    stop=True,
+                )
+
+        def doc_max(n):
+            nc.vector.tensor_reduce(out=mx[:, n : n + 1], in_=acc_t[n][:], axis=AX.X, op=ALU.max)
+
+        act_prog = [("aq",)]
+        for i in range(DOCS):
+            for c in range(TOK):
+                act_prog.append(("a", i, c))
+                if i == 0 and c == 0:
+                    act_prog.append(("rq",))
+                if c == 1 and i > 0 and group_of[i - 1] != group_of[i]:
+                    act_prog.append(("r", group_of[i - 1]))
+        act_prog.append(("r", groups - 1))
+
+        def act_step(op):
+            kind = op[0]
+            if kind == "a":
+                sumsq(op[1], op[2])
+            elif kind == "r":
+                inv_norm(op[1])
+            elif kind == "aq":
+                nc.scalar.activation(out=junkq[:], in_=xq[:], func=ACT.Square, accum_out=ssq[:])
+            else:
+                nc.scalar.activation(out=nrq[:], in_=ssq[:], func=ACT.Abs_reciprocal_sqrt, bias=tiny[:], scale=LIFT * LIFT)
+
+        def advance_act(marker):
+            while marker not in act_prog[: state["act"]]:
+                act_step(act_prog[state["act"]])
+                state["act"] = state["act"] + 1
+
+        nc.scalar.dma_start(out=xq[:], in_=x1.rearrange("b q k -> (b q) k"))
+        nc.scalar.dma_start(out=mrow[0:DOCS, :], in_=x2_mask.rearrange("b n s -> (b n) s"))
+        with nc.allow_non_contiguous_dma(reason="one 2-byte factor for each of 128 partitions"):
+            nc.scalar.dma_start(out=mq_bf[:], in_=x1_mask.rearrange("b (q o) -> (b q) o", o=1))
+        pump_loads()
+        nc.vector.memset(tiny[:], TINY)
+        nc.scalar.activation(out=warm[:], in_=tiny[:], func=ACT.Abs_reciprocal_sqrt, bias=tiny[:], scale=LIFT * LIFT)
+        make_identity(nc, identf[:])
+        nc.vector.memset(mrow[DOCS:P, :], 0.0)
+        nc.vector.memset(ga4[:].bitcast(I32), 0)
+        nc.vector.memset(blkm[:], 0.0)
+        for b in range(NB):
+            nc.vector.memset(blkm[b * LQ : (b + 1) * LQ, b : b + 1], 1.0)
+        nc.vector.tensor_copy(out=ident[:], in_=identf[:])
+        pm = misc_pool.tile([P, TOK, P], BF16, name="pm", tag="misc")
+        for c in range(TOK):
+            nc.tensor.transpose(pm[:, c, :], mrow[:, c : LD : TOK], ident[:])
+        nc.vector.tensor_scalar(
+            out=mk[:].rearrange("p (n b c) -> p n b c", b=NB, c=TOK),
+            in0=pm[:, :, 0:DOCS].rearrange("p c (b n) -> p n b c", b=NB),
+            scalar1=LIFT,
+            scalar2=None,
+            op0=ALU.mult,
+        )
+        nc.vector.tensor_scalar(out=mq[:], in0=mq_bf[:], scalar1=LIFT, scalar2=None, op0=ALU.mult)
+
+        def query_rows():
+            nc.vector.scalar_tensor_tensor(out=rmq[:], in0=nrq[:], scalar=GUARD, in1=mq[:], op0=ALU.min, op1=ALU.mult)
+            scaled(aq[:], xq[:], rmq[:])
+            pa = misc_pool.tile([P, 2, P], F32, name="pa", tag="misc")
+            words = aq[:].bitcast(F32)
+            for u in range(2):
+                nc.tensor.transpose(pa[:, u, :], words[:, u * P : (u + 1) * P], identf[:])
+            return pa
+
+        def query_codes(pa):
+            gaw = ga4[:].bitcast(F32).rearrange("p (b c u) -> p b c u", b=NB, u=2)
+            for b in range(NB):
+                qs = slice(b * LQ, (b + 1) * LQ)
+                nc.vector.tensor_copy(out=gaw[:, b, qs, :], in_=pa[:, :, qs].rearrange("p u c -> p c u"))
+            nc.vector.quantize_mx(out=a_codes[:].bitcast(FP8X4), scales=a_scl[:], in_=ga4[:])
+
+        advance_act(("rq",))
+        pa_tile = query_rows()
+
+        for i in range(DOCS + 2):
+            if i < DOCS:
+                g = group_of[i]
+                advance_act(("r", min(g + 1, groups - 1)))
+                if i == 0:
+                    row_factor(0)
+                scale_rows(i)
+                transposes(i)
+                pump_loads()
+            if i == 0:
+                query_codes(pa_tile)
+                spare["t"] = misc_pool.tile([P, LD], F32, name="spare", tag="misc")
+            if i >= 2:
+                quantise(i - 2)
+                product(i - 2)
+            if i + 1 < DOCS and group_of[i + 1] != group_of[i]:
+                row_factor(group_of[i + 1])
+            if 1 <= i <= DOCS:
+                evacuate(i - 1)
+            if i >= 2 and (i - 2) % NB == NB - 1:
+                doc_max((i - 2) // NB)
+
+        fin = misc_pool.tile([P, ND], F32, name="fin", tag="misc")
+        nc.tensor.matmul(out=fin[:], lhsT=blkm[:], rhs=mx[:], start=True, stop=True)
+        nc.vector.tensor_copy(out=res[:], in_=fin[:])
+        nc.sync.dma_start(out=out, in_=res[0:NB, :])

@@ -27,11 +27,12 @@ GUARD = 1e12 / LIFT
 
 FLOPS = 2 * NB * ND * LQ * LD * D
 
-GROUP_SIZES = [1, 1] + [2] * 31
+GROUP_SIZES = [1] * 4 + [2] * 28 + [1] * 4
 XR_BUFS = 14
 CLOCK_PASSES = 1
 SCALAR_SHARE = 8
-TAIL = 3
+SCALAR_TAIL = {DOCS - 3: (1,), DOCS - 2: (0, 1), DOCS - 1: (1,)}
+HEAD_DOCS = 4
 
 
 def tile_lateinteraction_kernel(tc, x1, x2, x1_mask, x2_mask, out):
@@ -77,6 +78,7 @@ def tile_lateinteraction_kernel(tc, x1, x2, x1_mask, x2_mask, out):
         a_codes = const.tile([P, NB * P], U32, name="a_codes", align_bytes=64)
         a_scl = const.tile([P, NB * P], U8, name="a_scl", align_bytes=64)
 
+        junkv_pool = ctx.enter_context(tc.tile_pool(name="junkv", bufs=2))
         xr_t = {}
         xs_t = {}
         pt_t = {}
@@ -98,7 +100,12 @@ def tile_lateinteraction_kernel(tc, x1, x2, x1_mask, x2_mask, out):
                 i = state["loads"]
                 b, n = doc_bn(i)
                 t = xr_pool.tile([P, TOK, D], BF16, name="xr")
-                nc.sync.dma_start(out=t[:], in_=x2[b, n].rearrange("(p c) f -> p c f", c=TOK))
+                src = x2[b, n].rearrange("(p c) f -> p c f", c=TOK)
+                if i == 0:
+                    for c in (0, 2, 1, 3):
+                        nc.sync.dma_start(out=t[:, c, :], in_=src[:, c, :])
+                else:
+                    nc.sync.dma_start(out=t[:], in_=src)
                 xr_t[i] = t
                 state["loads"] = i + 1
 
@@ -106,6 +113,14 @@ def tile_lateinteraction_kernel(tc, x1, x2, x1_mask, x2_mask, out):
             junk = junk_pool.tile([P, D], BF16, name="junk")
             col = i * TOK + c
             nc.scalar.activation(out=junk[:], in_=xr_t[i][:, c, :], func=ACT.Square, accum_out=ss_all[:, col : col + 1])
+
+        def sumsq_vector(i, c):
+            junkv = junkv_pool.tile([P, D], BF16, name="junkv")
+            col = i * TOK + c
+            x = xr_t[i][:, c, :]
+            nc.vector.scalar_tensor_tensor(
+                out=junkv[:], in0=x, scalar=1.0, in1=x, op0=ALU.mult, op1=ALU.mult, accum_out=ss_all[:, col : col + 1]
+            )
 
         def inv_norm(g):
             cols = cols_of(g)
@@ -148,7 +163,8 @@ def tile_lateinteraction_kernel(tc, x1, x2, x1_mask, x2_mask, out):
             for hb in range(2):
                 dst = gr[:, hb * 1024 : (hb + 1) * 1024].bitcast(F32).rearrange("p (c r u) -> p c r u", c=2, u=2)
                 src = pt_t[(i, hb)][:].rearrange("p c u r -> p c r u")
-                on_scalar = hb == 1 and (i % SCALAR_SHARE == SCALAR_SHARE - 1 or i >= DOCS - TAIL)
+                share = (1,) if i % SCALAR_SHARE == SCALAR_SHARE - 1 else ()
+                on_scalar = hb in SCALAR_TAIL.get(i, share)
                 if on_scalar:
                     nc.scalar.copy(out=dst, in_=src)
                 else:
@@ -176,7 +192,7 @@ def tile_lateinteraction_kernel(tc, x1, x2, x1_mask, x2_mask, out):
                 start=(b == 0),
                 stop=(b == NB - 1),
             )
-            for r in range(CLOCK_PASSES):
+            for r in range(CLOCK_PASSES if i < DOCS - 3 else 0):
                 nc.tensor.matmul_mx(
                     out=spare["t"][:],
                     lhsT=a_codes[:, bs].bitcast(FP8X4),
@@ -190,11 +206,13 @@ def tile_lateinteraction_kernel(tc, x1, x2, x1_mask, x2_mask, out):
         def doc_max(n):
             nc.vector.tensor_reduce(out=mx[:, n : n + 1], in_=acc_t[n][:], axis=AX.X, op=ALU.max)
 
-        act_prog = [("aq",)]
+        act_prog = []
         for i in range(DOCS):
-            for c in range(TOK):
+            for c in range(2 if i < HEAD_DOCS else TOK):
                 act_prog.append(("a", i, c))
-                if i == 0 and c == 0:
+                if i == 1 and c == 1:
+                    act_prog.append(("aq",))
+                if i == 2 and c == 1:
                     act_prog.append(("rq",))
                 if c == 1 and i > 0 and group_of[i - 1] != group_of[i]:
                     act_prog.append(("r", group_of[i - 1]))
@@ -216,8 +234,8 @@ def tile_lateinteraction_kernel(tc, x1, x2, x1_mask, x2_mask, out):
                 act_step(act_prog[state["act"]])
                 state["act"] = state["act"] + 1
 
-        nc.scalar.dma_start(out=xq[:], in_=x1.rearrange("b q k -> (b q) k"))
         nc.scalar.dma_start(out=mrow[0:DOCS, :], in_=x2_mask.rearrange("b n s -> (b n) s"))
+        nc.scalar.dma_start(out=xq[:], in_=x1.rearrange("b q k -> (b q) k"))
         with nc.allow_non_contiguous_dma(reason="one 2-byte factor for each of 128 partitions"):
             nc.scalar.dma_start(out=mq_bf[:], in_=x1_mask.rearrange("b (q o) -> (b q) o", o=1))
         pump_loads()
@@ -230,6 +248,8 @@ def tile_lateinteraction_kernel(tc, x1, x2, x1_mask, x2_mask, out):
         for b in range(NB):
             nc.vector.memset(blkm[b * LQ : (b + 1) * LQ, b : b + 1], 1.0)
         nc.vector.tensor_copy(out=ident[:], in_=identf[:])
+        sumsq_vector(0, 2)
+        sumsq_vector(0, 3)
         pm = misc_pool.tile([P, TOK, P], BF16, name="pm", tag="misc")
         for c in range(TOK):
             nc.tensor.transpose(pm[:, c, :], mrow[:, c : LD : TOK], ident[:])
@@ -258,19 +278,21 @@ def tile_lateinteraction_kernel(tc, x1, x2, x1_mask, x2_mask, out):
                 nc.vector.tensor_copy(out=gaw[:, b, qs, :], in_=pa[:, :, qs].rearrange("p u c -> p c u"))
             nc.vector.quantize_mx(out=a_codes[:].bitcast(FP8X4), scales=a_scl[:], in_=ga4[:])
 
-        advance_act(("rq",))
-        pa_tile = query_rows()
-
         for i in range(DOCS + 2):
             if i < DOCS:
                 g = group_of[i]
+                if i + 1 < HEAD_DOCS:
+                    sumsq_vector(i + 1, 2)
+                    sumsq_vector(i + 1, 3)
                 advance_act(("r", min(g + 1, groups - 1)))
                 if i == 0:
                     row_factor(0)
                 scale_rows(i)
                 transposes(i)
                 pump_loads()
-            if i == 0:
+            if i == 1:
+                advance_act(("rq",))
+                pa_tile = query_rows()
                 query_codes(pa_tile)
                 spare["t"] = misc_pool.tile([P, LD], F32, name="spare", tag="misc")
             if i >= 2:

@@ -29,10 +29,10 @@ FLOPS = 2 * NB * ND * LQ * LD * D
 
 GROUP_SIZES = [1] * 4 + [2] * 28 + [1] * 4
 XR_BUFS = 14
-CLOCK_PASSES = 1
+CLOCK_PASSES = 2
 SCALAR_SHARE = 8
 SCALAR_TAIL = {DOCS - 3: (1,), DOCS - 2: (0, 1), DOCS - 1: (1,)}
-HEAD_DOCS = 4
+HEAD_DOCS = 3
 
 
 def tile_lateinteraction_kernel(tc, x1, x2, x1_mask, x2_mask, out):
@@ -290,7 +290,7 @@ def tile_lateinteraction_kernel(tc, x1, x2, x1_mask, x2_mask, out):
                 scale_rows(i)
                 transposes(i)
                 pump_loads()
-            if i == 1:
+            if i == 2:
                 advance_act(("rq",))
                 pa_tile = query_rows()
                 query_codes(pa_tile)

@@ -30,7 +30,7 @@ FLOPS = 2 * NB * ND * LQ * LD * D
 GROUP_SIZES = [1] * 4 + [2] * 28 + [1] * 4
 XR_BUFS = 14
 CLOCK_PASSES = 2
-SCALAR_SHARE = 8
+GP_DOCS = range(3, DOCS - 1)
 SCALAR_TAIL = {DOCS - 3: (1,), DOCS - 2: (0, 1), DOCS - 1: (1,)}
 HEAD_DOCS = 3
 
@@ -78,9 +78,11 @@ def tile_lateinteraction_kernel(tc, x1, x2, x1_mask, x2_mask, out):
         a_codes = const.tile([P, NB * P], U32, name="a_codes", align_bytes=64)
         a_scl = const.tile([P, NB * P], U8, name="a_scl", align_bytes=64)
 
+        xg_pool = ctx.enter_context(tc.tile_pool(name="xg", bufs=1))
         junkv_pool = ctx.enter_context(tc.tile_pool(name="junkv", bufs=2))
         xr_t = {}
         xs_t = {}
+        xg_t = {}
         pt_t = {}
         gr_t = {}
         cd_t = {}
@@ -132,28 +134,38 @@ def tile_lateinteraction_kernel(tc, x1, x2, x1_mask, x2_mask, out):
                 out=rm_all[:, cols], in0=nr_all[:, cols], scalar=GUARD, in1=mk[:, cols], op0=ALU.min, op1=ALU.mult
             )
 
-        def scaled(out, in_, factor):
-            nc.vector.tensor_scalar(
+        def scaled(engine, out, in_, factor):
+            engine.tensor_scalar(
                 out=out.rearrange("p (u g e) -> p u g e", u=2, e=16),
                 in0=in_.rearrange("p (g u e) -> p u g e", u=2, e=16),
                 scalar1=factor,
-                scalar2=None,
+                scalar2=1.0,
                 op0=ALU.mult,
+                op1=ALU.mult,
             )
 
         def scale_rows(i):
             xs = work.tile([P, TOK, D], BF16, name="xs")
-            for c in range(TOK):
+            for c in range(TOK - 1 if i in GP_DOCS else TOK):
                 col = i * TOK + c
-                scaled(xs[:, c, :], xr_t[i][:, c, :], rm_all[:, col : col + 1])
+                scaled(nc.vector, xs[:, c, :], xr_t[i][:, c, :], rm_all[:, col : col + 1])
             xs_t[i] = xs
             state["b_done"] = i + 1
+
+        def scale_gpsimd(i):
+            if i in GP_DOCS:
+                col = i * TOK + TOK - 1
+                xg = xg_pool.tile([P, D], BF16, name="xg")
+                scaled(nc.gpsimd, xg[:], xr_t[i][:, TOK - 1, :], rm_all[:, col : col + 1])
+                xg_t[i] = xg
 
         def transposes(i):
             for hb in range(2):
                 pt = tp_pool.tile([P, 2, 2, P], F32, name="pt")
                 for cc in range(2):
-                    words = xs_t[i][:, 2 * hb + cc, :].bitcast(F32)
+                    c = 2 * hb + cc
+                    rows = xg_t[i][:] if c == TOK - 1 and i in GP_DOCS else xs_t[i][:, c, :]
+                    words = rows.bitcast(F32)
                     for u in range(2):
                         nc.tensor.transpose(pt[:, cc, u, :], words[:, u * P : (u + 1) * P], identf[:])
                 pt_t[(i, hb)] = pt
@@ -163,8 +175,7 @@ def tile_lateinteraction_kernel(tc, x1, x2, x1_mask, x2_mask, out):
             for hb in range(2):
                 dst = gr[:, hb * 1024 : (hb + 1) * 1024].bitcast(F32).rearrange("p (c r u) -> p c r u", c=2, u=2)
                 src = pt_t[(i, hb)][:].rearrange("p c u r -> p c r u")
-                share = (1,) if i % SCALAR_SHARE == SCALAR_SHARE - 1 else ()
-                on_scalar = hb in SCALAR_TAIL.get(i, share)
+                on_scalar = hb in SCALAR_TAIL.get(i, ())
                 if on_scalar:
                     nc.scalar.copy(out=dst, in_=src)
                 else:
@@ -264,7 +275,7 @@ def tile_lateinteraction_kernel(tc, x1, x2, x1_mask, x2_mask, out):
 
         def query_rows():
             nc.vector.scalar_tensor_tensor(out=rmq[:], in0=nrq[:], scalar=GUARD, in1=mq[:], op0=ALU.min, op1=ALU.mult)
-            scaled(aq[:], xq[:], rmq[:])
+            scaled(nc.vector, aq[:], xq[:], rmq[:])
             pa = misc_pool.tile([P, 2, P], F32, name="pa", tag="misc")
             words = aq[:].bitcast(F32)
             for u in range(2):
@@ -300,6 +311,8 @@ def tile_lateinteraction_kernel(tc, x1, x2, x1_mask, x2_mask, out):
                 product(i - 2)
             if i + 1 < DOCS and group_of[i + 1] != group_of[i]:
                 row_factor(group_of[i + 1])
+            if i + 1 < DOCS:
+                scale_gpsimd(i + 1)
             if 1 <= i <= DOCS:
                 evacuate(i - 1)
             if i >= 2 and (i - 2) % NB == NB - 1:

@@ -29,7 +29,7 @@ FLOPS = 2 * NB * ND * LQ * LD * D
 
 GROUP_SIZES = [1] * 4 + [2] * 28 + [1] * 4
 XR_BUFS = 14
-CLOCK_PASSES = 2
+CLOCK_PASSES = 3
 GP_DOCS = range(3, DOCS - 1)
 SCALAR_TAIL = {DOCS - 3: (1,), DOCS - 2: (0, 1), DOCS - 1: (1,)}
 HEAD_DOCS = 3

@@ -31,7 +31,7 @@ GROUP_SIZES = [1] * 4 + [2] * 28 + [1] * 4
 XR_BUFS = 14
 CLOCK_PASSES = 3
 GP_DOCS = range(3, DOCS - 1)
-SCALAR_TAIL = {DOCS - 3: (1,), DOCS - 2: (0, 1), DOCS - 1: (1,)}
+SCALAR_TAIL = {DOCS - 1: (1,), DOCS - 2: (0, 1,), DOCS - 3: (0, 1,), DOCS - 4: (0, 1,), DOCS - 5: (1,)}
 HEAD_DOCS = 3
 
 
@@ -47,7 +47,7 @@ def tile_lateinteraction_kernel(tc, x1, x2, x1_mask, x2_mask, out):
     with ExitStack() as ctx:
         const = ctx.enter_context(tc.tile_pool(name="const", bufs=1))
         xr_pool = ctx.enter_context(tc.tile_pool(name="xr", bufs=XR_BUFS))
-        work = ctx.enter_context(tc.tile_pool(name="work", bufs=3))
+        work = ctx.enter_context(tc.tile_pool(name="work", bufs=4))
         junk_pool = ctx.enter_context(tc.tile_pool(name="junk", bufs=4))
         tp_pool = ctx.enter_context(tc.psum_pool(name="tp", bufs=4))
         acc_pool = ctx.enter_context(tc.psum_pool(name="acc", bufs=2))
@@ -78,7 +78,7 @@ def tile_lateinteraction_kernel(tc, x1, x2, x1_mask, x2_mask, out):
         a_codes = const.tile([P, NB * P], U32, name="a_codes", align_bytes=64)
         a_scl = const.tile([P, NB * P], U8, name="a_scl", align_bytes=64)
 
-        xg_pool = ctx.enter_context(tc.tile_pool(name="xg", bufs=1))
+        xg_pool = ctx.enter_context(tc.tile_pool(name="xg", bufs=3))
         junkv_pool = ctx.enter_context(tc.tile_pool(name="junkv", bufs=2))
         xr_t = {}
         xs_t = {}
@@ -128,8 +128,8 @@ def tile_lateinteraction_kernel(tc, x1, x2, x1_mask, x2_mask, out):
             cols = cols_of(g)
             nc.scalar.activation(out=nr_all[:, cols], in_=ss_all[:, cols], func=ACT.Abs_reciprocal_sqrt, bias=tiny[:], scale=LIFT * LIFT)
 
-        def row_factor(g):
-            cols = cols_of(g)
+        def row_factor(i):
+            cols = slice(i * TOK, (i + 1) * TOK)
             nc.vector.scalar_tensor_tensor(
                 out=rm_all[:, cols], in0=nr_all[:, cols], scalar=GUARD, in1=mk[:, cols], op0=ALU.min, op1=ALU.mult
             )
@@ -289,7 +289,7 @@ def tile_lateinteraction_kernel(tc, x1, x2, x1_mask, x2_mask, out):
                 nc.vector.tensor_copy(out=gaw[:, b, qs, :], in_=pa[:, :, qs].rearrange("p u c -> p c u"))
             nc.vector.quantize_mx(out=a_codes[:].bitcast(FP8X4), scales=a_scl[:], in_=ga4[:])
 
-        for i in range(DOCS + 2):
+        for i in range(DOCS + 3):
             if i < DOCS:
                 g = group_of[i]
                 if i + 1 < HEAD_DOCS:
@@ -306,17 +306,18 @@ def tile_lateinteraction_kernel(tc, x1, x2, x1_mask, x2_mask, out):
                 pa_tile = query_rows()
                 query_codes(pa_tile)
                 spare["t"] = misc_pool.tile([P, LD], F32, name="spare", tag="misc")
-            if i >= 2:
+            if 2 <= i < DOCS + 2:
                 quantise(i - 2)
-                product(i - 2)
-            if i + 1 < DOCS and group_of[i + 1] != group_of[i]:
-                row_factor(group_of[i + 1])
+            if i >= 3:
+                product(i - 3)
+            if i + 1 < DOCS:
+                row_factor(i + 1)
             if i + 1 < DOCS:
                 scale_gpsimd(i + 1)
             if 1 <= i <= DOCS:
                 evacuate(i - 1)
-            if i >= 2 and (i - 2) % NB == NB - 1:
-                doc_max((i - 2) // NB)
+            if i >= 3 and (i - 3) % NB == NB - 1:
+                doc_max((i - 3) // NB)
 
         fin = misc_pool.tile([P, ND], F32, name="fin", tag="misc")
         nc.tensor.matmul(out=fin[:], lhsT=blkm[:], rhs=mx[:], start=True, stop=True)

@@ -30,7 +30,7 @@ FLOPS = 2 * NB * ND * LQ * LD * D
 GROUP_SIZES = [1] * 4 + [2] * 28 + [1] * 4
 XR_BUFS = 14
 CLOCK_PASSES = 3
-GP_DOCS = range(3, DOCS - 1)
+GP_DOCS = range(3, DOCS - 3)
 SCALAR_TAIL = {DOCS - 1: (1,), DOCS - 2: (0, 1,), DOCS - 3: (0, 1,), DOCS - 4: (0, 1,), DOCS - 5: (1,)}
 HEAD_DOCS = 3
 
@@ -78,7 +78,6 @@ def tile_lateinteraction_kernel(tc, x1, x2, x1_mask, x2_mask, out):
         a_codes = const.tile([P, NB * P], U32, name="a_codes", align_bytes=64)
         a_scl = const.tile([P, NB * P], U8, name="a_scl", align_bytes=64)
 
-        xg_pool = ctx.enter_context(tc.tile_pool(name="xg", bufs=3))
         junkv_pool = ctx.enter_context(tc.tile_pool(name="junkv", bufs=2))
         xr_t = {}
         xs_t = {}
@@ -103,7 +102,7 @@ def tile_lateinteraction_kernel(tc, x1, x2, x1_mask, x2_mask, out):
                 b, n = doc_bn(i)
                 t = xr_pool.tile([P, TOK, D], BF16, name="xr")
                 src = x2[b, n].rearrange("(p c) f -> p c f", c=TOK)
-                if i == 0:
+                if i < 2:
                     for c in (0, 2, 1, 3):
                         nc.sync.dma_start(out=t[:, c, :], in_=src[:, c, :])
                 else:
@@ -128,8 +127,8 @@ def tile_lateinteraction_kernel(tc, x1, x2, x1_mask, x2_mask, out):
             cols = cols_of(g)
             nc.scalar.activation(out=nr_all[:, cols], in_=ss_all[:, cols], func=ACT.Abs_reciprocal_sqrt, bias=tiny[:], scale=LIFT * LIFT)
 
-        def row_factor(i):
-            cols = slice(i * TOK, (i + 1) * TOK)
+        def row_factor(g):
+            cols = cols_of(g)
             nc.vector.scalar_tensor_tensor(
                 out=rm_all[:, cols], in0=nr_all[:, cols], scalar=GUARD, in1=mk[:, cols], op0=ALU.min, op1=ALU.mult
             )
@@ -155,8 +154,8 @@ def tile_lateinteraction_kernel(tc, x1, x2, x1_mask, x2_mask, out):
         def scale_gpsimd(i):
             if i in GP_DOCS:
                 col = i * TOK + TOK - 1
-                xg = xg_pool.tile([P, D], BF16, name="xg")
-                scaled(nc.gpsimd, xg[:], xr_t[i][:, TOK - 1, :], rm_all[:, col : col + 1])
+                xg = gr_t[i - 3][:, 0:D]
+                scaled(nc.gpsimd, xg, xr_t[i][:, TOK - 1, :], rm_all[:, col : col + 1])
                 xg_t[i] = xg
 
         def transposes(i):
@@ -164,7 +163,7 @@ def tile_lateinteraction_kernel(tc, x1, x2, x1_mask, x2_mask, out):
                 pt = tp_pool.tile([P, 2, 2, P], F32, name="pt")
                 for cc in range(2):
                     c = 2 * hb + cc
-                    rows = xg_t[i][:] if c == TOK - 1 and i in GP_DOCS else xs_t[i][:, c, :]
+                    rows = xg_t[i] if c == TOK - 1 and i in GP_DOCS else xs_t[i][:, c, :]
                     words = rows.bitcast(F32)
                     for u in range(2):
                         nc.tensor.transpose(pt[:, cc, u, :], words[:, u * P : (u + 1) * P], identf[:])
@@ -221,12 +220,12 @@ def tile_lateinteraction_kernel(tc, x1, x2, x1_mask, x2_mask, out):
         for i in range(DOCS):
             for c in range(2 if i < HEAD_DOCS else TOK):
                 act_prog.append(("a", i, c))
-                if i == 1 and c == 1:
+                if i == 3 and c == 0:
                     act_prog.append(("aq",))
-                if i == 2 and c == 1:
-                    act_prog.append(("rq",))
-                if c == 1 and i > 0 and group_of[i - 1] != group_of[i]:
+                if c == (0 if i < HEAD_DOCS else 1) and i > 0 and group_of[i - 1] != group_of[i]:
                     act_prog.append(("r", group_of[i - 1]))
+                if i == 3 and c == 1:
+                    act_prog.append(("rq",))
         act_prog.append(("r", groups - 1))
 
         def act_step(op):
@@ -298,20 +297,21 @@ def tile_lateinteraction_kernel(tc, x1, x2, x1_mask, x2_mask, out):
                 advance_act(("r", min(g + 1, groups - 1)))
                 if i == 0:
                     row_factor(0)
+                if i == 2:
+                    advance_act(("rq",))
+                    pa_tile = query_rows()
                 scale_rows(i)
                 transposes(i)
                 pump_loads()
             if i == 2:
-                advance_act(("rq",))
-                pa_tile = query_rows()
                 query_codes(pa_tile)
                 spare["t"] = misc_pool.tile([P, LD], F32, name="spare", tag="misc")
             if 2 <= i < DOCS + 2:
                 quantise(i - 2)
             if i >= 3:
                 product(i - 3)
-            if i + 1 < DOCS:
-                row_factor(i + 1)
+            if i + 1 < DOCS and group_of[i + 1] != group_of[i]:
+                row_factor(group_of[i + 1])
             if i + 1 < DOCS:
                 scale_gpsimd(i + 1)
             if 1 <= i <= DOCS:

@@ -32,6 +32,7 @@ XR_BUFS = 14
 CLOCK_PASSES = 3
 GP_DOCS = range(3, DOCS - 3)
 SCALAR_TAIL = {DOCS - 1: (1,), DOCS - 2: (0, 1,), DOCS - 3: (0, 1,), DOCS - 4: (0, 1,), DOCS - 5: (1,)}
+VECTOR_SUMS = (5,)
 HEAD_DOCS = 3
 
 
@@ -143,19 +144,26 @@ def tile_lateinteraction_kernel(tc, x1, x2, x1_mask, x2_mask, out):
                 op1=ALU.mult,
             )
 
+        def gp_tokens(i):
+            if i not in GP_DOCS:
+                return 0
+            return 2 if i % NB == 0 else 1
+
         def scale_rows(i):
             xs = work.tile([P, TOK, D], BF16, name="xs")
-            for c in range(TOK - 1 if i in GP_DOCS else TOK):
+            for c in range(TOK - gp_tokens(i)):
                 col = i * TOK + c
                 scaled(nc.vector, xs[:, c, :], xr_t[i][:, c, :], rm_all[:, col : col + 1])
             xs_t[i] = xs
             state["b_done"] = i + 1
 
         def scale_gpsimd(i):
-            if i in GP_DOCS:
-                col = i * TOK + TOK - 1
-                xg = gr_t[i - 3][:, 0:D]
-                scaled(nc.gpsimd, xg, xr_t[i][:, TOK - 1, :], rm_all[:, col : col + 1])
+            if gp_tokens(i) > 0:
+                xg = gr_t[i - 3]
+                for k in range(gp_tokens(i)):
+                    c = TOK - 1 - k
+                    col = i * TOK + c
+                    scaled(nc.gpsimd, xg[:, k * D : (k + 1) * D], xr_t[i][:, c, :], rm_all[:, col : col + 1])
                 xg_t[i] = xg
 
         def transposes(i):
@@ -163,7 +171,8 @@ def tile_lateinteraction_kernel(tc, x1, x2, x1_mask, x2_mask, out):
                 pt = tp_pool.tile([P, 2, 2, P], F32, name="pt")
                 for cc in range(2):
                     c = 2 * hb + cc
-                    rows = xg_t[i] if c == TOK - 1 and i in GP_DOCS else xs_t[i][:, c, :]
+                    k = TOK - 1 - c
+                    rows = xg_t[i][:, k * D : (k + 1) * D] if k < gp_tokens(i) else xs_t[i][:, c, :]
                     words = rows.bitcast(F32)
                     for u in range(2):
                         nc.tensor.transpose(pt[:, cc, u, :], words[:, u * P : (u + 1) * P], identf[:])
@@ -219,7 +228,8 @@ def tile_lateinteraction_kernel(tc, x1, x2, x1_mask, x2_mask, out):
         act_prog = []
         for i in range(DOCS):
             for c in range(2 if i < HEAD_DOCS else TOK):
-                act_prog.append(("a", i, c))
+                if c > 0 or i not in VECTOR_SUMS:
+                    act_prog.append(("a", i, c))
                 if i == 3 and c == 0:
                     act_prog.append(("aq",))
                 if c == (0 if i < HEAD_DOCS else 1) and i > 0 and group_of[i - 1] != group_of[i]:
@@ -288,9 +298,11 @@ def tile_lateinteraction_kernel(tc, x1, x2, x1_mask, x2_mask, out):
                 nc.vector.tensor_copy(out=gaw[:, b, qs, :], in_=pa[:, :, qs].rearrange("p u c -> p c u"))
             nc.vector.quantize_mx(out=a_codes[:].bitcast(FP8X4), scales=a_scl[:], in_=ga4[:])
 
-        for i in range(DOCS + 3):
+        for i in range(DOCS + 4):
             if i < DOCS:
                 g = group_of[i]
+                if i + 3 in VECTOR_SUMS:
+                    sumsq_vector(i + 3, 0)
                 if i + 1 < HEAD_DOCS:
                     sumsq_vector(i + 1, 2)
                     sumsq_vector(i + 1, 3)
@@ -308,7 +320,7 @@ def tile_lateinteraction_kernel(tc, x1, x2, x1_mask, x2_mask, out):
                 spare["t"] = misc_pool.tile([P, LD], F32, name="spare", tag="misc")
             if 2 <= i < DOCS + 2:
                 quantise(i - 2)
-            if i >= 3:
+            if 3 <= i < DOCS + 3:
                 product(i - 3)
             if i + 1 < DOCS and group_of[i + 1] != group_of[i]:
                 row_factor(group_of[i + 1])
@@ -316,8 +328,8 @@ def tile_lateinteraction_kernel(tc, x1, x2, x1_mask, x2_mask, out):
                 scale_gpsimd(i + 1)
             if 1 <= i <= DOCS:
                 evacuate(i - 1)
-            if i >= 3 and (i - 3) % NB == NB - 1:
-                doc_max((i - 3) // NB)
+            if 4 <= i and (i - 4) % NB == NB - 1:
+                doc_max((i - 4) // NB)
 
         fin = misc_pool.tile([P, ND], F32, name="fin", tag="misc")
         nc.tensor.matmul(out=fin[:], lhsT=blkm[:], rhs=mx[:], start=True, stop=True)

from contextlib import ExitStack

import concourse.mybir as mybir
from concourse.masks import make_identity

F32 = mybir.dt.float32
BF16 = mybir.dt.bfloat16
U8 = mybir.dt.uint8
U32 = mybir.dt.uint32
I32 = mybir.dt.int32
FP8X4 = mybir.dt.float8_e4m3fn_x4
ACT = mybir.ActivationFunctionType
ALU = mybir.AluOpType
AX = mybir.AxisListType

P = 128
NB = 4
ND = 16
LQ = 32
LD = 512
D = 512
DOCS = NB * ND
TOK = 4
LIFT = 128.0
TINY = 8e-27
GUARD = 1e12 / LIFT

FLOPS = 2 * NB * ND * LQ * LD * D

GROUP_SIZES = [1] * 4 + [2] * 28 + [1] * 4
XR_BUFS = 14
CLOCK_PASSES = 3
GP_DOCS = range(3, DOCS - 3)
SCALAR_TAIL = {DOCS - 1: (1,), DOCS - 2: (0, 1,), DOCS - 3: (0, 1,), DOCS - 4: (0, 1,), DOCS - 5: (1,)}
VECTOR_SUMS = (5,)
HEAD_DOCS = 3


def tile_lateinteraction_kernel(tc, x1, x2, x1_mask, x2_mask, out):
    nc = tc.nc
    first = []
    group_of = []
    for g, size in enumerate(GROUP_SIZES):
        first.append(len(group_of))
        group_of.extend([g] * size)
    groups = len(GROUP_SIZES)

    with ExitStack() as ctx:
        const = ctx.enter_context(tc.tile_pool(name="const", bufs=1))
        xr_pool = ctx.enter_context(tc.tile_pool(name="xr", bufs=XR_BUFS))
        work = ctx.enter_context(tc.tile_pool(name="work", bufs=4))
        junk_pool = ctx.enter_context(tc.tile_pool(name="junk", bufs=4))
        tp_pool = ctx.enter_context(tc.psum_pool(name="tp", bufs=4))
        acc_pool = ctx.enter_context(tc.psum_pool(name="acc", bufs=2))
        misc_pool = ctx.enter_context(tc.psum_pool(name="misc", bufs=1))
        ctx.enter_context(tc.manual_schedule())

        ident = const.tile([P, P], BF16, name="ident")
        identf = const.tile([P, P], F32, name="identf")
        blkm = const.tile([P, P], F32, name="blkm")
        tiny = const.tile([P, 1], F32, name="tiny")
        warm = const.tile([P, 1], F32, name="warm")
        ss_all = const.tile([P, DOCS * TOK], F32, name="ss_all")
        nr_all = const.tile([P, DOCS * TOK], F32, name="nr_all")
        rm_all = const.tile([P, DOCS * TOK], F32, name="rm_all")
        mk = const.tile([P, DOCS * TOK], F32, name="mk")
        mrow = const.tile([P, LD], BF16, name="mrow")
        mx = const.tile([P, ND], F32, name="mx")
        res = const.tile([P, ND], F32, name="res")
        xq = const.tile([P, D], BF16, name="xq")
        aq = const.tile([P, D], BF16, name="aq")
        junkq = const.tile([P, D], BF16, name="junkq")
        mq_bf = const.tile([P, 1], BF16, name="mq_bf")
        mq = const.tile([P, 1], F32, name="mq")
        ssq = const.tile([P, 1], F32, name="ssq")
        nrq = const.tile([P, 1], F32, name="nrq")
        rmq = const.tile([P, 1], F32, name="rmq")
        ga4 = const.tile([P, NB * P * 4], BF16, name="ga4", align_bytes=64)
        a_codes = const.tile([P, NB * P], U32, name="a_codes", align_bytes=64)
        a_scl = const.tile([P, NB * P], U8, name="a_scl", align_bytes=64)

        junkv_pool = ctx.enter_context(tc.tile_pool(name="junkv", bufs=2))
        xr_t = {}
        xs_t = {}
        xg_t = {}
        pt_t = {}
        gr_t = {}
        cd_t = {}
        sc_t = {}
        acc_t = {}
        spare = {}
        state = {"loads": 0, "b_done": 0, "act": 0}

        def doc_bn(i):
            return i % NB, i // NB

        def cols_of(g):
            return slice(first[g] * TOK, (first[g] + GROUP_SIZES[g]) * TOK)

        def pump_loads():
            while state["loads"] < min(DOCS, state["b_done"] + XR_BUFS):
                i = state["loads"]
                b, n = doc_bn(i)
                t = xr_pool.tile([P, TOK, D], BF16, name="xr")
                src = x2[b, n].rearrange("(p c) f -> p c f", c=TOK)
                if i < 2:
                    for c in (0, 2, 1, 3):
                        nc.sync.dma_start(out=t[:, c, :], in_=src[:, c, :])
                else:
                    nc.sync.dma_start(out=t[:], in_=src)
                xr_t[i] = t
                state["loads"] = i + 1

        def sumsq(i, c):
            junk = junk_pool.tile([P, D], BF16, name="junk")
            col = i * TOK + c
            nc.scalar.activation(out=junk[:], in_=xr_t[i][:, c, :], func=ACT.Square, accum_out=ss_all[:, col : col + 1])

        def sumsq_vector(i, c):
            junkv = junkv_pool.tile([P, D], BF16, name="junkv")
            col = i * TOK + c
            x = xr_t[i][:, c, :]
            nc.vector.scalar_tensor_tensor(
                out=junkv[:], in0=x, scalar=1.0, in1=x, op0=ALU.mult, op1=ALU.mult, accum_out=ss_all[:, col : col + 1]
            )

        def inv_norm(g):
            cols = cols_of(g)
            nc.scalar.activation(out=nr_all[:, cols], in_=ss_all[:, cols], func=ACT.Abs_reciprocal_sqrt, bias=tiny[:], scale=LIFT * LIFT)

        def row_factor(g):
            cols = cols_of(g)
            nc.vector.scalar_tensor_tensor(
                out=rm_all[:, cols], in0=nr_all[:, cols], scalar=GUARD, in1=mk[:, cols], op0=ALU.min, op1=ALU.mult
            )

        def scaled(engine, out, in_, factor):
            engine.tensor_scalar(
                out=out.rearrange("p (u g e) -> p u g e", u=2, e=16),
                in0=in_.rearrange("p (g u e) -> p u g e", u=2, e=16),
                scalar1=factor,
                scalar2=1.0,
                op0=ALU.mult,
                op1=ALU.mult,
            )

        def gp_tokens(i):
            if i not in GP_DOCS:
                return 0
            return 2 if i % NB == 0 else 1

        def scale_rows(i):
            xs = work.tile([P, TOK, D], BF16, name="xs")
            for c in range(TOK - gp_tokens(i)):
                col = i * TOK + c
                scaled(nc.vector, xs[:, c, :], xr_t[i][:, c, :], rm_all[:, col : col + 1])
            xs_t[i] = xs
            state["b_done"] = i + 1

        def scale_gpsimd(i):
            if gp_tokens(i) > 0:
                xg = gr_t[i - 3]
                for k in range(gp_tokens(i)):
                    c = TOK - 1 - k
                    col = i * TOK + c
                    scaled(nc.gpsimd, xg[:, k * D : (k + 1) * D], xr_t[i][:, c, :], rm_all[:, col : col + 1])
                xg_t[i] = xg

        def transposes(i):
            for hb in range(2):
                pt = tp_pool.tile([P, 2, 2, P], F32, name="pt")
                for cc in range(2):
                    c = 2 * hb + cc
                    k = TOK - 1 - c
                    rows = xg_t[i][:, k * D : (k + 1) * D] if k < gp_tokens(i) else xs_t[i][:, c, :]
                    words = rows.bitcast(F32)
                    for u in range(2):
                        nc.tensor.transpose(pt[:, cc, u, :], words[:, u * P : (u + 1) * P], identf[:])
                pt_t[(i, hb)] = pt

        def evacuate(i):
            gr = work.tile([P, 4 * LD], BF16, name="gr", align_bytes=64)
            for hb in range(2):
                dst = gr[:, hb * 1024 : (hb + 1) * 1024].bitcast(F32).rearrange("p (c r u) -> p c r u", c=2, u=2)
                src = pt_t[(i, hb)][:].rearrange("p c u r -> p c r u")
                on_scalar = hb in SCALAR_TAIL.get(i, ())
                if on_scalar:
                    nc.scalar.copy(out=dst, in_=src)
                else:
                    nc.vector.tensor_copy(out=dst, in_=src)
            gr_t[i] = gr

        def quantise(i):
            cd = work.tile([P, LD], U32, name="cd", align_bytes=64)
            sc = work.tile([P, LD], U8, name="sc", align_bytes=64)
            nc.vector.quantize_mx(out=cd[:].bitcast(FP8X4), scales=sc[:], in_=gr_t[i][:])
            cd_t[i] = cd
            sc_t[i] = sc

        def product(i):
            b, n = doc_bn(i)
            if b == 0:
                acc_t[n] = acc_pool.tile([P, LD], F32, name="acc")
            bs = slice(b * P, (b + 1) * P)
            nc.tensor.matmul_mx(
                out=acc_t[n][:],
                lhsT=a_codes[:, bs].bitcast(FP8X4),
                lhsT_scale=a_scl[:, bs],
                rhs=cd_t[i][:].bitcast(FP8X4),
                rhs_scale=sc_t[i][:],
                start=(b == 0),
                stop=(b == NB - 1),
            )
            for r in range(CLOCK_PASSES if i < DOCS - 3 else 0):
                nc.tensor.matmul_mx(
                    out=spare["t"][:],
                    lhsT=a_codes[:, bs].bitcast(FP8X4),
                    lhsT_scale=a_scl[:, bs],
                    rhs=cd_t[i][:].bitcast(FP8X4),
                    rhs_scale=sc_t[i][:],
                    start=True,
                    stop=True,
                )

        def doc_max(n):
            nc.vector.tensor_reduce(out=mx[:, n : n + 1], in_=acc_t[n][:], axis=AX.X, op=ALU.max)

        act_prog = []
        for i in range(DOCS):
            for c in range(2 if i < HEAD_DOCS else TOK):
                if c > 0 or i not in VECTOR_SUMS:
                    act_prog.append(("a", i, c))
                if i == 3 and c == 0:
                    act_prog.append(("aq",))
                if c == (0 if i < HEAD_DOCS else 1) and i > 0 and group_of[i - 1] != group_of[i]:
                    act_prog.append(("r", group_of[i - 1]))
                if i == 3 and c == 1:
                    act_prog.append(("rq",))
        act_prog.append(("r", groups - 1))

        def act_step(op):
            kind = op[0]
            if kind == "a":
                sumsq(op[1], op[2])
            elif kind == "r":
                inv_norm(op[1])
            elif kind == "aq":
                nc.scalar.activation(out=junkq[:], in_=xq[:], func=ACT.Square, accum_out=ssq[:])
            else:
                nc.scalar.activation(out=nrq[:], in_=ssq[:], func=ACT.Abs_reciprocal_sqrt, bias=tiny[:], scale=LIFT * LIFT)

        def advance_act(marker):
            while marker not in act_prog[: state["act"]]:
                act_step(act_prog[state["act"]])
                state["act"] = state["act"] + 1

        nc.scalar.dma_start(out=mrow[0:DOCS, :], in_=x2_mask.rearrange("b n s -> (b n) s"))
        nc.scalar.dma_start(out=xq[:], in_=x1.rearrange("b q k -> (b q) k"))
        with nc.allow_non_contiguous_dma(reason="one 2-byte factor for each of 128 partitions"):
            nc.scalar.dma_start(out=mq_bf[:], in_=x1_mask.rearrange("b (q o) -> (b q) o", o=1))
        pump_loads()
        nc.vector.memset(tiny[:], TINY)
        nc.scalar.activation(out=warm[:], in_=tiny[:], func=ACT.Abs_reciprocal_sqrt, bias=tiny[:], scale=LIFT * LIFT)
        make_identity(nc, identf[:])
        nc.vector.memset(mrow[DOCS:P, :], 0.0)
        nc.vector.memset(ga4[:].bitcast(I32), 0)
        nc.vector.memset(blkm[:], 0.0)
        for b in range(NB):
            nc.vector.memset(blkm[b * LQ : (b + 1) * LQ, b : b + 1], 1.0)
        nc.vector.tensor_copy(out=ident[:], in_=identf[:])
        sumsq_vector(0, 2)
        sumsq_vector(0, 3)
        pm = misc_pool.tile([P, TOK, P], BF16, name="pm", tag="misc")
        for c in range(TOK):
            nc.tensor.transpose(pm[:, c, :], mrow[:, c : LD : TOK], ident[:])
        nc.vector.tensor_scalar(
            out=mk[:].rearrange("p (n b c) -> p n b c", b=NB, c=TOK),
            in0=pm[:, :, 0:DOCS].rearrange("p c (b n) -> p n b c", b=NB),
            scalar1=LIFT,
            scalar2=None,
            op0=ALU.mult,
        )
        nc.vector.tensor_scalar(out=mq[:], in0=mq_bf[:], scalar1=LIFT, scalar2=None, op0=ALU.mult)

        def query_rows():
            nc.vector.scalar_tensor_tensor(out=rmq[:], in0=nrq[:], scalar=GUARD, in1=mq[:], op0=ALU.min, op1=ALU.mult)
            scaled(nc.vector, aq[:], xq[:], rmq[:])
            pa = misc_pool.tile([P, 2, P], F32, name="pa", tag="misc")
            words = aq[:].bitcast(F32)
            for u in range(2):
                nc.tensor.transpose(pa[:, u, :], words[:, u * P : (u + 1) * P], identf[:])
            return pa

        def query_codes(pa):
            gaw = ga4[:].bitcast(F32).rearrange("p (b c u) -> p b c u", b=NB, u=2)
            for b in range(NB):
                qs = slice(b * LQ, (b + 1) * LQ)
                nc.vector.tensor_copy(out=gaw[:, b, qs, :], in_=pa[:, :, qs].rearrange("p u c -> p c u"))
            nc.vector.quantize_mx(out=a_codes[:].bitcast(FP8X4), scales=a_scl[:], in_=ga4[:])

        for i in range(DOCS + 4):
            if i < DOCS:
                g = group_of[i]
                if i + 3 in VECTOR_SUMS:
                    sumsq_vector(i + 3, 0)
                if i + 1 < HEAD_DOCS:
                    sumsq_vector(i + 1, 2)
                    sumsq_vector(i + 1, 3)
                advance_act(("r", min(g + 1, groups - 1)))
                if i == 0:
                    row_factor(0)
                if i == 2:
                    advance_act(("rq",))
                    pa_tile = query_rows()
                scale_rows(i)
                transposes(i)
                pump_loads()
            if i == 2:
                query_codes(pa_tile)
                spare["t"] = misc_pool.tile([P, LD], F32, name="spare", tag="misc")
            if 2 <= i < DOCS + 2:
                quantise(i - 2)
            if 3 <= i < DOCS + 3:
                product(i - 3)
            if i + 1 < DOCS and group_of[i + 1] != group_of[i]:
                row_factor(group_of[i + 1])
            if i + 1 < DOCS:
                scale_gpsimd(i + 1)
            if 1 <= i <= DOCS:
                evacuate(i - 1)
            if 4 <= i and (i - 4) % NB == NB - 1:
                doc_max((i - 4) // NB)

        fin = misc_pool.tile([P, ND], F32, name="fin", tag="misc")
        nc.tensor.matmul(out=fin[:], lhsT=blkm[:], rhs=mx[:], start=True, stop=True)
        nc.vector.tensor_copy(out=res[:], in_=fin[:])
        nc.sync.dma_start(out=out, in_=res[0:NB, :])
